import numpy as np
import ml_dtypes


def mxq(x, axis, fmt="e4m3"):
    dtype, down = {"e4m3": (ml_dtypes.float8_e4m3fn, 7), "e5m2": (ml_dtypes.float8_e5m2, 14)}[fmt]
    v = np.moveaxis(np.asarray(x, np.float32).astype(ml_dtypes.bfloat16).astype(np.float64), axis, -1)
    blocks = v.reshape(v.shape[:-1] + (-1, 32))
    amax = np.abs(blocks).max(-1, keepdims=True)
    byte = np.maximum(np.where(amax > 0, np.frexp(amax)[1] - 1 + 127, 0) - down, 1)
    scale = np.exp2(byte - 127.0)
    codes = (blocks / scale).astype(np.float32).astype(dtype).astype(np.float64)
    return np.moveaxis((codes * scale).reshape(v.shape), -1, axis)


WIDE = False


def mx_kscale(k):
    if not WIDE:
        return np.ones(k)
    levels = np.array([10, -10, 5, -5, 0])
    if k % 512:
        return np.exp2(np.random.permutation(np.resize(levels, k // 32))).repeat(32)
    a = np.empty((k // 512, 16))
    for p in range(k // 512):
        a[p, :8] = np.random.permutation(np.resize(levels, 8))
        for g in range(8):
            far = levels[np.abs(levels - a[p, g]) >= 10]
            a[p, g + 8] = far[np.random.randint(len(far))]
    return np.exp2(a.ravel()).repeat(32)


BF16 = ml_dtypes.bfloat16


def bf(x):
    return np.asarray(x, np.float32).astype(BF16)


def f64(x):
    return np.asarray(x).astype(np.float64)


B, L, D, F = 128, 8, 512, 1024
EPS = 1e-12


def l2norm(w, axis):
    n = np.sqrt(np.sum(w * w, axis=axis, keepdims=True))
    return w / np.maximum(n, EPS)


def silu(z):
    return z / (1.0 + np.exp(-z))


def draw_w(k, n, s):
    a = np.random.standard_normal((L, k, n)) / s[:, None]
    return a / np.sqrt(np.sum(a * a, axis=1, keepdims=True)) * np.exp2(np.random.randint(-1, 2, (L, 1, n)))


def draw_gain():
    return np.random.choice([-1.0, 1.0], (1, F)) * (1.0 + 0.1 * np.random.standard_normal((1, F)))


def setup_inputs():
    s, t = mx_kscale(D), mx_kscale(F)
    c = np.sqrt(np.mean(1.0 / s**2))
    return {'x': bf(np.random.standard_normal((B, L, D)) * s),
            'W_gate': bf(draw_w(D, F, s)),
            'W_up': bf(draw_w(D, F, s)),
            'W_down': bf(draw_w(F, D, t)),
            's_u': bf(draw_gain() * c * t),
            's_v': bf(draw_gain() * c * 1.5 / np.sqrt(D))}


def reference(x, W_gate, W_up, W_down, s_u, s_v):
    Wg = l2norm(f64(W_gate), 1)
    Wu = l2norm(f64(W_up), 1)
    Wd = l2norm(f64(W_down), 1)
    xq = mxq(f64(x), 2, 'e4m3').transpose(1, 0, 2)
    u = xq @ mxq(Wg, 1, 'e4m3')
    v = xq @ mxq(Wu, 1, 'e4m3')
    u_scale = np.abs(f64(s_u)) * 1.0
    v_scale = np.abs(f64(s_v)) * np.sqrt(D)
    h = silu(v_scale * v) * (u_scale * u)
    out = (mxq(h, 2, 'e4m3') @ mxq(Wd, 1, 'e4m3')).transpose(1, 0, 2)
    return l2norm(out, -1)

@@ -1,0 +1,245 @@
+from contextlib import ExitStack
+import math
+
+import concourse.mybir as mybir
+from concourse.masks import make_identity
+
+B, L, D, F = 128, 8, 512, 1024
+FLOPS = 2 * B * L * (2 * D * F + F * D)
+
+F32 = mybir.dt.float32
+BF16 = mybir.dt.bfloat16
+U32 = mybir.dt.uint32
+U8 = mybir.dt.uint8
+FP8X4 = mybir.dt.float8_e4m3fn_x4
+ACT = mybir.ActivationFunctionType
+ALU = mybir.AluOpType
+
+P = 128
+EPS_SQ = 1e-24
+UV_DT = F32
+LEAD = 2
+
+
+def tile_npertokenswishglu_kernel(tc, x, W_gate, W_up, W_down, s_u, s_v, out):
+    nc = tc.nc
+    with ExitStack() as ctx:
+        const = ctx.enter_context(tc.tile_pool(name="const", bufs=1))
+        rawp = ctx.enter_context(tc.tile_pool(name="rawp", bufs=6))
+        grpp = ctx.enter_context(tc.tile_pool(name="grpp", bufs=3))
+        codep = ctx.enter_context(tc.tile_pool(name="codep", bufs=8))
+        small = ctx.enter_context(tc.tile_pool(name="small", bufs=6))
+        junkp = ctx.enter_context(tc.tile_pool(name="junkp", bufs=2))
+        ep = ctx.enter_context(tc.tile_pool(name="ep", bufs=2))
+        psum = ctx.enter_context(tc.psum_pool(name="psum", bufs=1))
+
+        ident = const.tile([P, P], F32, name="ident")
+        make_identity(nc, ident[:])
+        mhalf = const.tile([P, 8], F32, name="mhalf")
+        nc.gpsimd.memset(mhalf[:], -0.5)
+        warm = const.tile([P, 1], F32, name="warm")
+        nc.scalar.activation(out=warm[:], in_=mhalf[:, 0:1], func=ACT.Silu)
+
+        raws = {}
+
+        def load_unit(i):
+            l, mat = divmod(i, 3)
+            raw = rawp.tile([P, 4096], BF16, name="raw", tag="raw")
+            if i == 0:
+                for b in range(4):
+                    nc.sync.dma_start(
+                        out=raw[:].rearrange("p (j c) -> p j c", j=4)[:, :, 256 * b : 256 * (b + 1)],
+                        in_=W_gate[l].rearrange("(p j) c -> p j c", j=4)[:, :, 256 * b : 256 * (b + 1)],
+                    )
+            elif mat < 2:
+                w = W_gate if mat == 0 else W_up
+                nc.sync.dma_start(
+                    out=raw[:].rearrange("p (j c) -> p j c", j=4),
+                    in_=w[l].rearrange("(p j) c -> p j c", j=4),
+                )
+            else:
+                nc.sync.dma_start(
+                    out=raw[:].rearrange("p (h j c) -> p h j c", h=2, j=4),
+                    in_=W_down[l].rearrange("(h p j) c -> p h j c", h=2, j=4),
+                )
+            raws[i] = raw
+
+        load_unit(0)
+
+        x_sb = const.tile([P, L * D], BF16, name="x_sb")
+        nc.sync.dma_start(out=x_sb[:].rearrange("p (l d) -> p l d", l=L), in_=x)
+        su_raw = const.tile([P, 8], BF16, name="su_raw")
+        sv_raw = const.tile([P, 8], BF16, name="sv_raw")
+        nc.sync.dma_start(out=su_raw[:].rearrange("p (g t) -> p g t", g=2), in_=s_u.rearrange("o (g p t) -> p (o g) t", g=2, t=4))
+        nc.sync.dma_start(out=sv_raw[:].rearrange("p (g t) -> p g t", g=2), in_=s_v.rearrange("o (g p t) -> p (o g) t", g=2, t=4))
+        us = const.tile([P, 8], F32, name="us")
+        vs = const.tile([P, 8], F32, name="vs")
+        nc.scalar.activation(out=us[:], in_=su_raw[:], func=ACT.Abs)
+        nc.scalar.activation(out=vs[:], in_=sv_raw[:], func=ACT.Abs, scale=math.sqrt(D))
+
+        load_unit(1)
+        load_unit(2)
+        load_unit(3)
+
+        def rsqrt_cols(dst, src):
+            n = src.shape[1]
+            clamped = small.tile([P, 8], F32, name="clamped", tag="clamped")
+            nc.gpsimd.tensor_scalar(out=clamped[:, 0:n], in0=src, scalar1=EPS_SQ, scalar2=None, op0=ALU.max)
+            nc.gpsimd.tensor_tensor(out=dst, in0=clamped[:, 0:n], in1=mhalf[:, 0:n], op=ALU.pow)
+
+        def norms(i):
+            mat = i % 3
+            words = raws[i][:].bitcast(F32)
+            nsq = small.tile([P, 8], F32, name="nsq", tag="nsq")
+            rn = small.tile([P, 8], F32, name="rn", tag="rn")
+            for bank in range(4):
+                wt = psum.tile([P, 4, P], F32, name="wt", tag="wt", bufs=3)
+                hi, lo = divmod(bank, 2)
+                for j in range(4):
+                    if mat < 2:
+                        off = 512 * j + 128 * bank
+                    else:
+                        off = 1024 * lo + 256 * j + 128 * hi
+                    nc.tensor.transpose(wt[:, j, :], words[:, off : off + 128], ident[:])
+                halves = wt[:].rearrange("p j q -> p (j q)").bitcast(BF16).rearrange("p (n e) -> p e n", e=2)
+                for e in range(2):
+                    if mat < 2:
+                        col = 4 * hi + 2 * e + lo
+                    else:
+                        col = 4 * lo + 2 * e + hi
+                    junk = junkp.tile([P, 512], BF16, name="junk", tag="junk")
+                    nc.scalar.activation(out=junk[:], in_=halves[:, e, :], func=ACT.Square, accum_out=nsq[:, col : col + 1])
+                if mat < 2 and lo == 1:
+                    rsqrt_cols(rn[:, 4 * hi : 4 * hi + 4], nsq[:, 4 * hi : 4 * hi + 4])
+            if mat == 2:
+                tot = small.tile([P, 4], F32, name="tot", tag="tot")
+                nc.gpsimd.tensor_tensor(out=tot[:], in0=nsq[:, 0:4], in1=nsq[:, 4:8], op=ALU.add)
+                rsqrt_cols(rn[:, 0:4], tot[:])
+            return rn
+
+        def spread(rn, c0):
+            rnb = psum.tile([P, 512], F32, name="rnb", tag="rnb", bufs=2)
+            for k in range(4):
+                nc.tensor.transpose(rnb[:, 128 * k : 128 * (k + 1)], rn[:, c0 + k : c0 + k + 1].to_broadcast([P, P]), ident[:])
+            return rnb
+
+        def quantise(grp):
+            codes = codep.tile([P, 512], U32, name="wcodes", tag="wcodes", align_bytes=64)
+            scales = codep.tile([P, 512], U8, name="wscales", tag="wscales", align_bytes=64)
+            nc.vector.quantize_mx(out=codes[:].bitcast(FP8X4), scales=scales[:], in_=grp[:])
+            return codes, scales
+
+        def scale_stage1(i, blk, rnb):
+            grp = grpp.tile([P, 2048], BF16, name="grp", tag="grp", align_bytes=64)
+            rv = raws[i][:].rearrange("p (j c) -> p j c", j=4)[:, :, 512 * blk : 512 * (blk + 1)]
+            rv = rv.rearrange("p j (m a e) -> p e a m j", a=2, e=2)
+            gv = grp[:].rearrange("p (a e m j) -> p e a m j", a=2, e=2, j=4)
+            bv = rnb[:].rearrange("p (e m a) -> p e a m", e=2, a=2)
+            for e in range(2):
+                nc.vector.tensor_tensor(
+                    out=gv[:, e], in0=rv[:, e], in1=bv[:, e].unsqueeze(3).to_broadcast([P, 2, P, 4]), op=ALU.mult
+                )
+            return grp
+
+        def scale_stage2(i, h, rnb):
+            grp = grpp.tile([P, 2048], BF16, name="grp", tag="grp", align_bytes=64)
+            rv = raws[i][:].rearrange("p (h j c) -> p h j c", h=2, j=4)[:, h]
+            rv = rv.rearrange("p j (c e) -> p c e j", e=2)
+            gv = grp[:].rearrange("p (c e j) -> p c e j", e=2, j=4)
+            bv = rnb[:].rearrange("p (e c) -> p c e", e=2).unsqueeze(3).to_broadcast([P, 256, 2, 4])
+            nc.vector.tensor_tensor(out=gv, in0=rv, in1=bv, op=ALU.mult)
+            return grp
+
+        rns = {}
+        rns[0] = norms(0)
+
+        xw = x_sb[:].bitcast(F32)
+        xg = const.tile([P, L * D], BF16, name="xg", align_bytes=64)
+        xgw = xg[:].bitcast(F32)
+        for lp in range(L // 2):
+            xt = psum.tile([P, 4, P], F32, name="xt", tag="wt", bufs=3)
+            for l2 in range(2):
+                for u in range(2):
+                    l = 2 * lp + l2
+                    nc.tensor.transpose(xt[:, 2 * l2 + u, :], xw[:, 256 * l + u : 256 * (l + 1) : 2], ident[:])
+            nc.vector.tensor_copy(
+                out=xgw[:, 512 * lp : 512 * (lp + 1)].rearrange("p (a n u) -> p a n u", a=2, u=2),
+                in_=xt[:].rearrange("p (a u) n -> p a n u", a=2),
+            )
+        x_codes = const.tile([P, L * P], U32, name="x_codes", align_bytes=64)
+        x_scales = const.tile([P, L * P], U8, name="x_scales", align_bytes=64)
+        nc.vector.quantize_mx(out=x_codes[:].bitcast(FP8X4), scales=x_scales[:], in_=xg[:])
+
+        for i in range(1, LEAD):
+            rns[i] = norms(i)
+        for l in range(L):
+            q = {}
+            hg = ep.tile([P, 1024], BF16, name="hg", tag="hg", align_bytes=64)
+            for mat in range(3):
+                i = 3 * l + mat
+                if i + 4 < 3 * L:
+                    load_unit(i + 4)
+                if i + LEAD < 3 * L:
+                    rns[i + LEAD] = norms(i + LEAD)
+                rn = rns[i]
+                if mat == 2:
+                    rnb = spread(rn, 0)
+                for half in range(2):
+                    if mat < 2:
+                        rnb = spread(rn, 4 * half)
+                        grp = scale_stage1(i, half, rnb)
+                    else:
+                        grp = scale_stage2(i, half, rnb)
+                    q[(mat, half)] = quantise(grp)
+                    if mat == 1:
+                        g = half
+                        u_ps = psum.tile([P, 4, P], UV_DT, name="u_ps", tag="uv", bufs=2)
+                        v_ps = psum.tile([P, 4, P], UV_DT, name="v_ps", tag="uv", bufs=2)
+                        for dst, m in ((v_ps, 1), (u_ps, 0)):
+                            codes, scales = q[(m, g)]
+                            for t in range(4):
+                                nc.tensor.matmul_mx(
+                                    out=dst[:, t, :],
+                                    lhsT=codes[:, 128 * t : 128 * (t + 1)].bitcast(FP8X4),
+                                    lhsT_scale=scales[:, 128 * t : 128 * (t + 1)],
+                                    rhs=x_codes[:, 128 * l : 128 * (l + 1)].bitcast(FP8X4),
+                                    rhs_scale=x_scales[:, 128 * l : 128 * (l + 1)],
+                                    start=True,
+                                    stop=True,
+                                )
+                        s1 = ep.tile([P, 4, P], F32, name="s1", tag="s1")
+                        for t in range(4):
+                            nc.scalar.activation(out=s1[:, t, :], in_=v_ps[:, t, :], func=ACT.Silu, scale=vs[:, 4 * g + t : 4 * g + t + 1])
+                        h_t = ep.tile([P, 4, P], BF16, name="h_t", tag="h_t")
+                        for t in range(4):
+                            nc.vector.scalar_tensor_tensor(
+                                out=h_t[:, t, :], in0=u_ps[:, t, :], scalar=us[:, 4 * g + t : 4 * g + t + 1], in1=s1[:, t, :],
+                                op0=ALU.mult, op1=ALU.mult,
+                            )
+                        nc.scalar.copy(
+                            out=hg[:, 512 * g : 512 * (g + 1)].rearrange("p (n t) -> p n t", t=4),
+                            in_=h_t[:].rearrange("p t n -> p n t"),
+                        )
+            h_codes = ep.tile([P, 256], U32, name="h_codes", tag="h_codes", align_bytes=64)
+            h_scales = ep.tile([P, 256], U8, name="h_scales", tag="h_scales", align_bytes=64)
+            nc.vector.quantize_mx(out=h_codes[:].bitcast(FP8X4), scales=h_scales[:], in_=hg[:])
+            o_ps = psum.tile([P, 512], F32, name="o_ps", tag="o", bufs=1)
+            for g in range(2):
+                codes, scales = q[(2, g)]
+                nc.tensor.matmul_mx(
+                    out=o_ps[:],
+                    lhsT=h_codes[:, 128 * g : 128 * (g + 1)].bitcast(FP8X4),
+                    lhsT_scale=h_scales[:, 128 * g : 128 * (g + 1)],
+                    rhs=codes[:].bitcast(FP8X4),
+                    rhs_scale=scales[:],
+                    start=(g == 0),
+                    stop=(g == 1),
+                )
+            ss = small.tile([P, 1], F32, name="ss", tag="ss")
+            junk = junkp.tile([P, 512], BF16, name="junk", tag="junk")
+            nc.scalar.activation(out=junk[:], in_=o_ps[:], func=ACT.Square, accum_out=ss[:])
+            rno = small.tile([P, 1], F32, name="rno", tag="rno")
+            rsqrt_cols(rno[:], ss[:])
+            o_sb = ep.tile([P, 512], F32, name="o_sb", tag="o_sb")
+            nc.scalar.activation(out=o_sb[:], in_=o_ps[:], func=ACT.Copy, scale=rno[:, 0:1])
+            nc.sync.dma_start(out=out[:, l, :], in_=o_sb[:])

@@ -27,7 +27,7 @@ def tile_npertokenswishglu_kernel(tc, x, W_gate, W_up, W_down, s_u, s_v, out):
         const = ctx.enter_context(tc.tile_pool(name="const", bufs=1))
         rawp = ctx.enter_context(tc.tile_pool(name="rawp", bufs=6))
         grpp = ctx.enter_context(tc.tile_pool(name="grpp", bufs=3))
-        codep = ctx.enter_context(tc.tile_pool(name="codep", bufs=8))
+        codep = ctx.enter_context(tc.tile_pool(name="codep", bufs=5))
         small = ctx.enter_context(tc.tile_pool(name="small", bufs=6))
         junkp = ctx.enter_context(tc.tile_pool(name="junkp", bufs=2))
         ep = ctx.enter_context(tc.tile_pool(name="ep", bufs=2))
@@ -39,6 +39,11 @@ def tile_npertokenswishglu_kernel(tc, x, W_gate, W_up, W_down, s_u, s_v, out):
         nc.gpsimd.memset(mhalf[:], -0.5)
         warm = const.tile([P, 1], F32, name="warm")
         nc.scalar.activation(out=warm[:], in_=mhalf[:, 0:1], func=ACT.Silu)
+
+        su_raw = const.tile([P, 8], BF16, name="su_raw")
+        sv_raw = const.tile([P, 8], BF16, name="sv_raw")
+        nc.scalar.dma_start(out=su_raw[:].rearrange("p (g t) -> p g t", g=2), in_=s_u.rearrange("o (g p t) -> p (o g) t", g=2, t=4))
+        nc.scalar.dma_start(out=sv_raw[:].rearrange("p (g t) -> p g t", g=2), in_=s_v.rearrange("o (g p t) -> p (o g) t", g=2, t=4))
 
         raws = {}
 
@@ -68,15 +73,6 @@ def tile_npertokenswishglu_kernel(tc, x, W_gate, W_up, W_down, s_u, s_v, out):
 
         x_sb = const.tile([P, L * D], BF16, name="x_sb")
         nc.sync.dma_start(out=x_sb[:].rearrange("p (l d) -> p l d", l=L), in_=x)
-        su_raw = const.tile([P, 8], BF16, name="su_raw")
-        sv_raw = const.tile([P, 8], BF16, name="sv_raw")
-        nc.sync.dma_start(out=su_raw[:].rearrange("p (g t) -> p g t", g=2), in_=s_u.rearrange("o (g p t) -> p (o g) t", g=2, t=4))
-        nc.sync.dma_start(out=sv_raw[:].rearrange("p (g t) -> p g t", g=2), in_=s_v.rearrange("o (g p t) -> p (o g) t", g=2, t=4))
-        us = const.tile([P, 8], F32, name="us")
-        vs = const.tile([P, 8], F32, name="vs")
-        nc.scalar.activation(out=us[:], in_=su_raw[:], func=ACT.Abs)
-        nc.scalar.activation(out=vs[:], in_=sv_raw[:], func=ACT.Abs, scale=math.sqrt(D))
-
         load_unit(1)
         load_unit(2)
         load_unit(3)
@@ -123,115 +119,95 @@ def tile_npertokenswishglu_kernel(tc, x, W_gate, W_up, W_down, s_u, s_v, out):
                 nc.tensor.transpose(rnb[:, 128 * k : 128 * (k + 1)], rn[:, c0 + k : c0 + k + 1].to_broadcast([P, P]), ident[:])
             return rnb
 
-        def quantise(grp):
-            codes = codep.tile([P, 512], U32, name="wcodes", tag="wcodes", align_bytes=64)
-            scales = codep.tile([P, 512], U8, name="wscales", tag="wscales", align_bytes=64)
-            nc.vector.quantize_mx(out=codes[:].bitcast(FP8X4), scales=scales[:], in_=grp[:])
-            return codes, scales
-
-        def scale_stage1(i, blk, rnb):
-            grp = grpp.tile([P, 2048], BF16, name="grp", tag="grp", align_bytes=64)
-            rv = raws[i][:].rearrange("p (j c) -> p j c", j=4)[:, :, 512 * blk : 512 * (blk + 1)]
-            rv = rv.rearrange("p j (m a e) -> p e a m j", a=2, e=2)
-            gv = grp[:].rearrange("p (a e m j) -> p e a m j", a=2, e=2, j=4)
-            bv = rnb[:].rearrange("p (e m a) -> p e a m", e=2, a=2)
-            for e in range(2):
-                nc.vector.tensor_tensor(
-                    out=gv[:, e], in0=rv[:, e], in1=bv[:, e].unsqueeze(3).to_broadcast([P, 2, P, 4]), op=ALU.mult
-                )
-            return grp
-
-        def scale_stage2(i, h, rnb):
-            grp = grpp.tile([P, 2048], BF16, name="grp", tag="grp", align_bytes=64)
-            rv = raws[i][:].rearrange("p (h j c) -> p h j c", h=2, j=4)[:, h]
-            rv = rv.rearrange("p j (c e) -> p c e j", e=2)
-            gv = grp[:].rearrange("p (c e j) -> p c e j", e=2, j=4)
-            bv = rnb[:].rearrange("p (e c) -> p c e", e=2).unsqueeze(3).to_broadcast([P, 256, 2, 4])
-            nc.vector.tensor_tensor(out=gv, in0=rv, in1=bv, op=ALU.mult)
-            return grp
-
         rns = {}
-        rns[0] = norms(0)
+        grps = {}
+        codes = {}
+        scales = {}
+        rnbs = {}
 
-        xw = x_sb[:].bitcast(F32)
-        xg = const.tile([P, L * D], BF16, name="xg", align_bytes=64)
-        xgw = xg[:].bitcast(F32)
-        for lp in range(L // 2):
-            xt = psum.tile([P, 4, P], F32, name="xt", tag="wt", bufs=3)
-            for l2 in range(2):
-                for u in range(2):
-                    l = 2 * lp + l2
-                    nc.tensor.transpose(xt[:, 2 * l2 + u, :], xw[:, 256 * l + u : 256 * (l + 1) : 2], ident[:])
-            nc.vector.tensor_copy(
-                out=xgw[:, 512 * lp : 512 * (lp + 1)].rearrange("p (a n u) -> p a n u", a=2, u=2),
-                in_=xt[:].rearrange("p (a u) n -> p a n u", a=2),
+        def prefetch(i):
+            if 4 <= i + 4 < 3 * L:
+                load_unit(i + 4)
+            if LEAD <= i + LEAD < 3 * L:
+                rns[i + LEAD] = norms(i + LEAD)
+
+        def scale(i, half):
+            mat = i % 3
+            if half == 0:
+                grps[i] = grpp.tile([P, 4096], BF16, name="grp", tag="grp", align_bytes=64)
+                codes[i] = codep.tile([P, 1024], U32, name="wcodes", tag="wcodes", align_bytes=64)
+                scales[i] = codep.tile([P, 1024], U8, name="wscales", tag="wscales", align_bytes=64)
+            chunk = raws[i][:, 2048 * half : 2048 * (half + 1)] if mat == 2 else None
+            dst = grps[i][:, 2048 * half : 2048 * (half + 1)]
+            if mat < 2:
+                rnb = spread(rns[i], 4 * half)
+                rv = raws[i][:].rearrange("p (j c) -> p j c", j=4)[:, :, 512 * half : 512 * (half + 1)]
+                rv = rv.rearrange("p j (m a e) -> p m a e j", a=2, e=2)
+                gv = dst.rearrange("p (a e m j) -> p m a e j", a=2, e=2, j=4)
+                bv = rnb[:].rearrange("p (e m a) -> p m a e", e=2, a=2).unsqueeze(4).to_broadcast([P, P, 2, 2, 4])
+            else:
+                if half == 0:
+                    rnbs[i] = spread(rns[i], 0)
+                rnb = rnbs[i]
+                rv = chunk.rearrange("p (j c e) -> p c e j", j=4, e=2)
+                gv = dst.rearrange("p (c e j) -> p c e j", e=2, j=4)
+                bv = rnb[:].rearrange("p (e c) -> p c e", e=2).unsqueeze(3).to_broadcast([P, 256, 2, 4])
+            nc.vector.tensor_tensor(out=gv, in0=rv, in1=bv, op=ALU.mult)
+
+        def quantise(i, lo, hi):
+            nc.vector.quantize_mx(
+                out=codes[i][:, lo // 4 : hi // 4].bitcast(FP8X4), scales=scales[i][:, lo // 4 : hi // 4], in_=grps[i][:, lo:hi]
             )
-        x_codes = const.tile([P, L * P], U32, name="x_codes", align_bytes=64)
-        x_scales = const.tile([P, L * P], U8, name="x_scales", align_bytes=64)
-        nc.vector.quantize_mx(out=x_codes[:].bitcast(FP8X4), scales=x_scales[:], in_=xg[:])
 
-        for i in range(1, LEAD):
-            rns[i] = norms(i)
-        for l in range(L):
-            q = {}
-            hg = ep.tile([P, 1024], BF16, name="hg", tag="hg", align_bytes=64)
-            for mat in range(3):
-                i = 3 * l + mat
-                if i + 4 < 3 * L:
-                    load_unit(i + 4)
-                if i + LEAD < 3 * L:
-                    rns[i + LEAD] = norms(i + LEAD)
-                rn = rns[i]
-                if mat == 2:
-                    rnb = spread(rn, 0)
-                for half in range(2):
-                    if mat < 2:
-                        rnb = spread(rn, 4 * half)
-                        grp = scale_stage1(i, half, rnb)
-                    else:
-                        grp = scale_stage2(i, half, rnb)
-                    q[(mat, half)] = quantise(grp)
-                    if mat == 1:
-                        g = half
-                        u_ps = psum.tile([P, 4, P], UV_DT, name="u_ps", tag="uv", bufs=2)
-                        v_ps = psum.tile([P, 4, P], UV_DT, name="v_ps", tag="uv", bufs=2)
-                        for dst, m in ((v_ps, 1), (u_ps, 0)):
-                            codes, scales = q[(m, g)]
-                            for t in range(4):
-                                nc.tensor.matmul_mx(
-                                    out=dst[:, t, :],
-                                    lhsT=codes[:, 128 * t : 128 * (t + 1)].bitcast(FP8X4),
-                                    lhsT_scale=scales[:, 128 * t : 128 * (t + 1)],
-                                    rhs=x_codes[:, 128 * l : 128 * (l + 1)].bitcast(FP8X4),
-                                    rhs_scale=x_scales[:, 128 * l : 128 * (l + 1)],
-                                    start=True,
-                                    stop=True,
-                                )
-                        s1 = ep.tile([P, 4, P], F32, name="s1", tag="s1")
-                        for t in range(4):
-                            nc.scalar.activation(out=s1[:, t, :], in_=v_ps[:, t, :], func=ACT.Silu, scale=vs[:, 4 * g + t : 4 * g + t + 1])
-                        h_t = ep.tile([P, 4, P], BF16, name="h_t", tag="h_t")
-                        for t in range(4):
-                            nc.vector.scalar_tensor_tensor(
-                                out=h_t[:, t, :], in0=u_ps[:, t, :], scalar=us[:, 4 * g + t : 4 * g + t + 1], in1=s1[:, t, :],
-                                op0=ALU.mult, op1=ALU.mult,
-                            )
-                        nc.scalar.copy(
-                            out=hg[:, 512 * g : 512 * (g + 1)].rearrange("p (n t) -> p n t", t=4),
-                            in_=h_t[:].rearrange("p t n -> p n t"),
-                        )
+        uv = {}
+        hgs = {}
+
+        def stage1(l, g):
+            u_ps = psum.tile([P, 4, P], UV_DT, name="u_ps", tag="uv", bufs=2)
+            v_ps = psum.tile([P, 4, P], UV_DT, name="v_ps", tag="uv", bufs=2)
+            for dst, i in ((v_ps, 3 * l + 1), (u_ps, 3 * l)):
+                for t in range(4):
+                    cols = slice(512 * g + 128 * t, 512 * g + 128 * (t + 1))
+                    nc.tensor.matmul_mx(
+                        out=dst[:, t, :],
+                        lhsT=codes[i][:, cols].bitcast(FP8X4),
+                        lhsT_scale=scales[i][:, cols],
+                        rhs=x_codes[:, 128 * l : 128 * (l + 1)].bitcast(FP8X4),
+                        rhs_scale=x_scales[:, 128 * l : 128 * (l + 1)],
+                        start=True,
+                        stop=True,
+                    )
+            s1 = ep.tile([P, 4, P], F32, name="s1", tag="s1")
+            for t in range(4):
+                nc.scalar.activation(out=s1[:, t, :], in_=v_ps[:, t, :], func=ACT.Silu, scale=vs[:, 4 * g + t : 4 * g + t + 1])
+            uv[(l, g)] = (u_ps, s1)
+
+        def hidden(l, g):
+            u_ps, s1 = uv[(l, g)]
+            h_t = ep.tile([P, 4, P], BF16, name="h_t", tag="h_t")
+            for t in range(4):
+                nc.vector.scalar_tensor_tensor(
+                    out=h_t[:, t, :], in0=u_ps[:, t, :], scalar=us[:, 4 * g + t : 4 * g + t + 1], in1=s1[:, t, :],
+                    op0=ALU.mult, op1=ALU.mult,
+                )
+            nc.scalar.copy(
+                out=hgs[l][:, 512 * g : 512 * (g + 1)].rearrange("p (n t) -> p n t", t=4),
+                in_=h_t[:].rearrange("p t n -> p n t"),
+            )
+
+        def down(l):
+            i = 3 * l + 2
             h_codes = ep.tile([P, 256], U32, name="h_codes", tag="h_codes", align_bytes=64)
             h_scales = ep.tile([P, 256], U8, name="h_scales", tag="h_scales", align_bytes=64)
-            nc.vector.quantize_mx(out=h_codes[:].bitcast(FP8X4), scales=h_scales[:], in_=hg[:])
+            nc.vector.quantize_mx(out=h_codes[:].bitcast(FP8X4), scales=h_scales[:], in_=hgs[l][:])
             o_ps = psum.tile([P, 512], F32, name="o_ps", tag="o", bufs=1)
             for g in range(2):
-                codes, scales = q[(2, g)]
                 nc.tensor.matmul_mx(
                     out=o_ps[:],
                     lhsT=h_codes[:, 128 * g : 128 * (g + 1)].bitcast(FP8X4),
                     lhsT_scale=h_scales[:, 128 * g : 128 * (g + 1)],
-                    rhs=codes[:].bitcast(FP8X4),
-                    rhs_scale=scales[:],
+                    rhs=codes[i][:, 512 * g : 512 * (g + 1)].bitcast(FP8X4),
+                    rhs_scale=scales[i][:, 512 * g : 512 * (g + 1)],
                     start=(g == 0),
                     stop=(g == 1),
                 )
@@ -243,3 +219,55 @@ def tile_npertokenswishglu_kernel(tc, x, W_gate, W_up, W_down, s_u, s_v, out):
             o_sb = ep.tile([P, 512], F32, name="o_sb", tag="o_sb")
             nc.scalar.activation(out=o_sb[:], in_=o_ps[:], func=ACT.Copy, scale=rno[:, 0:1])
             nc.sync.dma_start(out=out[:, l, :], in_=o_sb[:])
+
+        rns[0] = norms(0)
+
+        xw = x_sb[:].bitcast(F32)
+        xg = const.tile([P, L * D], BF16, name="xg", align_bytes=64)
+        xgw = xg[:].bitcast(F32)
+        for lp in range(L // 2):
+            xt = psum.tile([P, 4, P], F32, name="xt", tag="wt", bufs=3)
+            for l2 in range(2):
+                for u in range(2):
+                    l = 2 * lp + l2
+                    nc.tensor.transpose(xt[:, 2 * l2 + u, :], xw[:, 256 * l + u : 256 * (l + 1) : 2], ident[:])
+            nc.scalar.copy(
+                out=xgw[:, 512 * lp : 512 * (lp + 1)].rearrange("p (a n u) -> p a n u", a=2, u=2),
+                in_=xt[:].rearrange("p (a u) n -> p a n u", a=2),
+            )
+        us = const.tile([P, 8], F32, name="us")
+        vs = const.tile([P, 8], F32, name="vs")
+        nc.scalar.activation(out=us[:], in_=su_raw[:], func=ACT.Abs)
+        nc.scalar.activation(out=vs[:], in_=sv_raw[:], func=ACT.Abs, scale=math.sqrt(D))
+        x_codes = const.tile([P, L * P], U32, name="x_codes", align_bytes=64)
+        x_scales = const.tile([P, L * P], U8, name="x_scales", align_bytes=64)
+
+        for i in range(1, LEAD):
+            rns[i] = norms(i)
+
+        with tc.manual_schedule(engines={mybir.EngineType.DVE}):
+            for l in range(L):
+                ig, iu, idn = 3 * l, 3 * l + 1, 3 * l + 2
+                hgs[l] = ep.tile([P, 1024], BF16, name="hg", tag="hg", align_bytes=64)
+                prefetch(ig)
+                scale(ig, 0)
+                if l > 0:
+                    down(l - 1)
+                scale(ig, 1)
+                prefetch(iu)
+                scale(iu, 0)
+                quantise(ig, 0, 4096)
+                if l == 0:
+                    nc.vector.quantize_mx(out=x_codes[:].bitcast(FP8X4), scales=x_scales[:], in_=xg[:])
+                scale(iu, 1)
+                quantise(iu, 0, 2048)
+                stage1(l, 0)
+                quantise(iu, 2048, 4096)
+                prefetch(idn)
+                scale(idn, 0)
+                hidden(l, 0)
+                stage1(l, 1)
+                scale(idn, 1)
+                hidden(l, 1)
+                quantise(idn, 0, 4096)
+            down(L - 1)

from contextlib import ExitStack
import math

import concourse.mybir as mybir
from concourse.masks import make_identity

B, L, D, F = 128, 8, 512, 1024
FLOPS = 2 * B * L * (2 * D * F + F * D)

F32 = mybir.dt.float32
BF16 = mybir.dt.bfloat16
U32 = mybir.dt.uint32
U8 = mybir.dt.uint8
FP8X4 = mybir.dt.float8_e4m3fn_x4
ACT = mybir.ActivationFunctionType
ALU = mybir.AluOpType

P = 128
EPS_SQ = 1e-24
UV_DT = F32
LEAD = 2


def tile_npertokenswishglu_kernel(tc, x, W_gate, W_up, W_down, s_u, s_v, out):
    nc = tc.nc
    with ExitStack() as ctx:
        const = ctx.enter_context(tc.tile_pool(name="const", bufs=1))
        rawp = ctx.enter_context(tc.tile_pool(name="rawp", bufs=6))
        grpp = ctx.enter_context(tc.tile_pool(name="grpp", bufs=3))
        codep = ctx.enter_context(tc.tile_pool(name="codep", bufs=5))
        small = ctx.enter_context(tc.tile_pool(name="small", bufs=6))
        junkp = ctx.enter_context(tc.tile_pool(name="junkp", bufs=2))
        ep = ctx.enter_context(tc.tile_pool(name="ep", bufs=2))
        psum = ctx.enter_context(tc.psum_pool(name="psum", bufs=1))

        ident = const.tile([P, P], F32, name="ident")
        make_identity(nc, ident[:])
        mhalf = const.tile([P, 8], F32, name="mhalf")
        nc.gpsimd.memset(mhalf[:], -0.5)
        warm = const.tile([P, 1], F32, name="warm")
        nc.scalar.activation(out=warm[:], in_=mhalf[:, 0:1], func=ACT.Silu)

        su_raw = const.tile([P, 8], BF16, name="su_raw")
        sv_raw = const.tile([P, 8], BF16, name="sv_raw")
        nc.scalar.dma_start(out=su_raw[:].rearrange("p (g t) -> p g t", g=2), in_=s_u.rearrange("o (g p t) -> p (o g) t", g=2, t=4))
        nc.scalar.dma_start(out=sv_raw[:].rearrange("p (g t) -> p g t", g=2), in_=s_v.rearrange("o (g p t) -> p (o g) t", g=2, t=4))

        raws = {}

        def load_unit(i):
            l, mat = divmod(i, 3)
            raw = rawp.tile([P, 4096], BF16, name="raw", tag="raw")
            if i == 0:
                for b in range(4):
                    nc.sync.dma_start(
                        out=raw[:].rearrange("p (j c) -> p j c", j=4)[:, :, 256 * b : 256 * (b + 1)],
                        in_=W_gate[l].rearrange("(p j) c -> p j c", j=4)[:, :, 256 * b : 256 * (b + 1)],
                    )
            elif mat < 2:
                w = W_gate if mat == 0 else W_up
                nc.sync.dma_start(
                    out=raw[:].rearrange("p (j c) -> p j c", j=4),
                    in_=w[l].rearrange("(p j) c -> p j c", j=4),
                )
            else:
                nc.sync.dma_start(
                    out=raw[:].rearrange("p (h j c) -> p h j c", h=2, j=4),
                    in_=W_down[l].rearrange("(h p j) c -> p h j c", h=2, j=4),
                )
            raws[i] = raw

        load_unit(0)

        x_sb = const.tile([P, L * D], BF16, name="x_sb")
        nc.sync.dma_start(out=x_sb[:].rearrange("p (l d) -> p l d", l=L), in_=x)
        load_unit(1)
        load_unit(2)
        load_unit(3)

        def rsqrt_cols(dst, src):
            n = src.shape[1]
            clamped = small.tile([P, 8], F32, name="clamped", tag="clamped")
            nc.gpsimd.tensor_scalar(out=clamped[:, 0:n], in0=src, scalar1=EPS_SQ, scalar2=None, op0=ALU.max)
            nc.gpsimd.tensor_tensor(out=dst, in0=clamped[:, 0:n], in1=mhalf[:, 0:n], op=ALU.pow)

        def norms(i):
            mat = i % 3
            words = raws[i][:].bitcast(F32)
            nsq = small.tile([P, 8], F32, name="nsq", tag="nsq")
            rn = small.tile([P, 8], F32, name="rn", tag="rn")
            for bank in range(4):
                wt = psum.tile([P, 4, P], F32, name="wt", tag="wt", bufs=3)
                hi, lo = divmod(bank, 2)
                for j in range(4):
                    if mat < 2:
                        off = 512 * j + 128 * bank
                    else:
                        off = 1024 * lo + 256 * j + 128 * hi
                    nc.tensor.transpose(wt[:, j, :], words[:, off : off + 128], ident[:])
                halves = wt[:].rearrange("p j q -> p (j q)").bitcast(BF16).rearrange("p (n e) -> p e n", e=2)
                for e in range(2):
                    if mat < 2:
                        col = 4 * hi + 2 * e + lo
                    else:
                        col = 4 * lo + 2 * e + hi
                    junk = junkp.tile([P, 512], BF16, name="junk", tag="junk")
                    nc.scalar.activation(out=junk[:], in_=halves[:, e, :], func=ACT.Square, accum_out=nsq[:, col : col + 1])
                if mat < 2 and lo == 1:
                    rsqrt_cols(rn[:, 4 * hi : 4 * hi + 4], nsq[:, 4 * hi : 4 * hi + 4])
            if mat == 2:
                tot = small.tile([P, 4], F32, name="tot", tag="tot")
                nc.gpsimd.tensor_tensor(out=tot[:], in0=nsq[:, 0:4], in1=nsq[:, 4:8], op=ALU.add)
                rsqrt_cols(rn[:, 0:4], tot[:])
            return rn

        def spread(rn, c0):
            rnb = psum.tile([P, 512], F32, name="rnb", tag="rnb", bufs=2)
            for k in range(4):
                nc.tensor.transpose(rnb[:, 128 * k : 128 * (k + 1)], rn[:, c0 + k : c0 + k + 1].to_broadcast([P, P]), ident[:])
            return rnb

        rns = {}
        grps = {}
        codes = {}
        scales = {}
        rnbs = {}

        def prefetch(i):
            if 4 <= i + 4 < 3 * L:
                load_unit(i + 4)
            if LEAD <= i + LEAD < 3 * L:
                rns[i + LEAD] = norms(i + LEAD)

        def scale(i, half):
            mat = i % 3
            if half == 0:
                grps[i] = grpp.tile([P, 4096], BF16, name="grp", tag="grp", align_bytes=64)
                codes[i] = codep.tile([P, 1024], U32, name="wcodes", tag="wcodes", align_bytes=64)
                scales[i] = codep.tile([P, 1024], U8, name="wscales", tag="wscales", align_bytes=64)
            chunk = raws[i][:, 2048 * half : 2048 * (half + 1)] if mat == 2 else None
            dst = grps[i][:, 2048 * half : 2048 * (half + 1)]
            if mat < 2:
                rnb = spread(rns[i], 4 * half)
                rv = raws[i][:].rearrange("p (j c) -> p j c", j=4)[:, :, 512 * half : 512 * (half + 1)]
                rv = rv.rearrange("p j (m a e) -> p m a e j", a=2, e=2)
                gv = dst.rearrange("p (a e m j) -> p m a e j", a=2, e=2, j=4)
                bv = rnb[:].rearrange("p (e m a) -> p m a e", e=2, a=2).unsqueeze(4).to_broadcast([P, P, 2, 2, 4])
            else:
                if half == 0:
                    rnbs[i] = spread(rns[i], 0)
                rnb = rnbs[i]
                rv = chunk.rearrange("p (j c e) -> p c e j", j=4, e=2)
                gv = dst.rearrange("p (c e j) -> p c e j", e=2, j=4)
                bv = rnb[:].rearrange("p (e c) -> p c e", e=2).unsqueeze(3).to_broadcast([P, 256, 2, 4])
            nc.vector.tensor_tensor(out=gv, in0=rv, in1=bv, op=ALU.mult)

        def quantise(i, lo, hi):
            nc.vector.quantize_mx(
                out=codes[i][:, lo // 4 : hi // 4].bitcast(FP8X4), scales=scales[i][:, lo // 4 : hi // 4], in_=grps[i][:, lo:hi]
            )

        uv = {}
        hgs = {}

        def stage1(l, g):
            u_ps = psum.tile([P, 4, P], UV_DT, name="u_ps", tag="uv", bufs=2)
            v_ps = psum.tile([P, 4, P], UV_DT, name="v_ps", tag="uv", bufs=2)
            for dst, i in ((v_ps, 3 * l + 1), (u_ps, 3 * l)):
                for t in range(4):
                    cols = slice(512 * g + 128 * t, 512 * g + 128 * (t + 1))
                    nc.tensor.matmul_mx(
                        out=dst[:, t, :],
                        lhsT=codes[i][:, cols].bitcast(FP8X4),
                        lhsT_scale=scales[i][:, cols],
                        rhs=x_codes[:, 128 * l : 128 * (l + 1)].bitcast(FP8X4),
                        rhs_scale=x_scales[:, 128 * l : 128 * (l + 1)],
                        start=True,
                        stop=True,
                    )
            s1 = ep.tile([P, 4, P], F32, name="s1", tag="s1")
            for t in range(4):
                nc.scalar.activation(out=s1[:, t, :], in_=v_ps[:, t, :], func=ACT.Silu, scale=vs[:, 4 * g + t : 4 * g + t + 1])
            uv[(l, g)] = (u_ps, s1)

        def hidden(l, g):
            u_ps, s1 = uv[(l, g)]
            h_t = ep.tile([P, 4, P], BF16, name="h_t", tag="h_t")
            for t in range(4):
                nc.vector.scalar_tensor_tensor(
                    out=h_t[:, t, :], in0=u_ps[:, t, :], scalar=us[:, 4 * g + t : 4 * g + t + 1], in1=s1[:, t, :],
                    op0=ALU.mult, op1=ALU.mult,
                )
            nc.scalar.copy(
                out=hgs[l][:, 512 * g : 512 * (g + 1)].rearrange("p (n t) -> p n t", t=4),
                in_=h_t[:].rearrange("p t n -> p n t"),
            )

        def down(l):
            i = 3 * l + 2
            h_codes = ep.tile([P, 256], U32, name="h_codes", tag="h_codes", align_bytes=64)
            h_scales = ep.tile([P, 256], U8, name="h_scales", tag="h_scales", align_bytes=64)
            nc.vector.quantize_mx(out=h_codes[:].bitcast(FP8X4), scales=h_scales[:], in_=hgs[l][:])
            o_ps = psum.tile([P, 512], F32, name="o_ps", tag="o", bufs=1)
            for g in range(2):
                nc.tensor.matmul_mx(
                    out=o_ps[:],
                    lhsT=h_codes[:, 128 * g : 128 * (g + 1)].bitcast(FP8X4),
                    lhsT_scale=h_scales[:, 128 * g : 128 * (g + 1)],
                    rhs=codes[i][:, 512 * g : 512 * (g + 1)].bitcast(FP8X4),
                    rhs_scale=scales[i][:, 512 * g : 512 * (g + 1)],
                    start=(g == 0),
                    stop=(g == 1),
                )
            ss = small.tile([P, 1], F32, name="ss", tag="ss")
            junk = junkp.tile([P, 512], BF16, name="junk", tag="junk")
            nc.scalar.activation(out=junk[:], in_=o_ps[:], func=ACT.Square, accum_out=ss[:])
            rno = small.tile([P, 1], F32, name="rno", tag="rno")
            rsqrt_cols(rno[:], ss[:])
            o_sb = ep.tile([P, 512], F32, name="o_sb", tag="o_sb")
            nc.scalar.activation(out=o_sb[:], in_=o_ps[:], func=ACT.Copy, scale=rno[:, 0:1])
            nc.sync.dma_start(out=out[:, l, :], in_=o_sb[:])

        rns[0] = norms(0)

        xw = x_sb[:].bitcast(F32)
        xg = const.tile([P, L * D], BF16, name="xg", align_bytes=64)
        xgw = xg[:].bitcast(F32)
        for lp in range(L // 2):
            xt = psum.tile([P, 4, P], F32, name="xt", tag="wt", bufs=3)
            for l2 in range(2):
                for u in range(2):
                    l = 2 * lp + l2
                    nc.tensor.transpose(xt[:, 2 * l2 + u, :], xw[:, 256 * l + u : 256 * (l + 1) : 2], ident[:])
            nc.scalar.copy(
                out=xgw[:, 512 * lp : 512 * (lp + 1)].rearrange("p (a n u) -> p a n u", a=2, u=2),
                in_=xt[:].rearrange("p (a u) n -> p a n u", a=2),
            )
        us = const.tile([P, 8], F32, name="us")
        vs = const.tile([P, 8], F32, name="vs")
        nc.scalar.activation(out=us[:], in_=su_raw[:], func=ACT.Abs)
        nc.scalar.activation(out=vs[:], in_=sv_raw[:], func=ACT.Abs, scale=math.sqrt(D))
        x_codes = const.tile([P, L * P], U32, name="x_codes", align_bytes=64)
        x_scales = const.tile([P, L * P], U8, name="x_scales", align_bytes=64)

        for i in range(1, LEAD):
            rns[i] = norms(i)

        with tc.manual_schedule(engines={mybir.EngineType.DVE}):
            for l in range(L):
                ig, iu, idn = 3 * l, 3 * l + 1, 3 * l + 2
                hgs[l] = ep.tile([P, 1024], BF16, name="hg", tag="hg", align_bytes=64)
                prefetch(ig)
                scale(ig, 0)
                if l > 0:
                    down(l - 1)
                scale(ig, 1)
                prefetch(iu)
                scale(iu, 0)
                quantise(ig, 0, 4096)
                if l == 0:
                    nc.vector.quantize_mx(out=x_codes[:].bitcast(FP8X4), scales=x_scales[:], in_=xg[:])
                scale(iu, 1)
                quantise(iu, 0, 2048)
                stage1(l, 0)
                quantise(iu, 2048, 4096)
                prefetch(idn)
                scale(idn, 0)
                hidden(l, 0)
                stage1(l, 1)
                scale(idn, 1)
                hidden(l, 1)
                quantise(idn, 0, 4096)
            down(L - 1)
